import numpy as np
import ml_dtypes


def mxq(x, axis, fmt="e4m3"):
    dtype, down = {"e4m3": (ml_dtypes.float8_e4m3fn, 7), "e5m2": (ml_dtypes.float8_e5m2, 14)}[fmt]
    v = np.moveaxis(np.asarray(x, np.float32).astype(ml_dtypes.bfloat16).astype(np.float64), axis, -1)
    blocks = v.reshape(v.shape[:-1] + (-1, 32))
    amax = np.abs(blocks).max(-1, keepdims=True)
    byte = np.maximum(np.where(amax > 0, np.frexp(amax)[1] - 1 + 127, 0) - down, 1)
    scale = np.exp2(byte - 127.0)
    codes = (blocks / scale).astype(np.float32).astype(dtype).astype(np.float64)
    return np.moveaxis((codes * scale).reshape(v.shape), -1, axis)


WIDE = False


def mx_kscale(k):
    if not WIDE:
        return np.ones(k)
    levels = np.array([10, -10, 5, -5, 0])
    if k % 512:
        return np.exp2(np.random.permutation(np.resize(levels, k // 32))).repeat(32)
    a = np.empty((k // 512, 16))
    for p in range(k // 512):
        a[p, :8] = np.random.permutation(np.resize(levels, 8))
        for g in range(8):
            far = levels[np.abs(levels - a[p, g]) >= 10]
            a[p, g + 8] = far[np.random.randint(len(far))]
    return np.exp2(a.ravel()).repeat(32)


BF16 = ml_dtypes.bfloat16


def bf(x):
    return np.asarray(x, np.float32).astype(BF16)


def f64(x):
    return np.asarray(x).astype(np.float64)


B, T, N, D, L = 4, 8, 128, 1024, 512


def setup_inputs():
    s, r = mx_kscale(D), mx_kscale(L)
    x = np.random.standard_normal((B, T, N, D)) + 0.5 * np.random.standard_normal(D)
    return {"x": bf(x * s),
            "Wtheta": bf(np.random.standard_normal((L, D)) / np.sqrt(D) / s * r[:, None]),
            "Wphi": bf(np.random.standard_normal((L, D)) / np.sqrt(D) / s / r[:, None])}


def reference(x, Wtheta, Wphi):
    xq = mxq(f64(x), 3, "e4m3")
    th = xq @ mxq(f64(Wtheta), 1, "e4m3").T
    ph = xq @ mxq(f64(Wphi), 1, "e4m3").T
    thq, phq = mxq(th, 3, "e4m3"), mxq(ph, 3, "e4m3")
    sw = (thq @ phq.transpose(0, 1, 3, 2)) / N
    tw = (thq.transpose(0, 2, 1, 3) @ phq.transpose(0, 2, 3, 1)).transpose(0, 2, 1, 3) / T
    return sw, tw

@@ -1,0 +1,281 @@
+from contextlib import ExitStack
+
+import concourse.masks as masks
+import concourse.mybir as mybir
+
+F32 = mybir.dt.float32
+BF16 = mybir.dt.bfloat16
+U32 = mybir.dt.uint32
+I32 = mybir.dt.int32
+U8 = mybir.dt.uint8
+FP8X4 = mybir.dt.float8_e4m3fn_x4
+ALU = mybir.AluOpType
+AX = mybir.AxisListType
+
+P = 128
+B, T, N, D, L = 4, 8, 128, 1024, 512
+FRAMES = B * T
+QUADS = FRAMES // 4
+HA = 8
+LATE = 3
+FLOPS = 2 * 2 * FRAMES * N * D * L + 2 * FRAMES * N * N * L + 2 * B * N * T * T * L
+
+
+def tile_higcin_volleyball_pa_t_kernel(tc, x, Wtheta, Wphi, out_0, out_1):
+    nc = tc.nc
+    with ExitStack() as ctx:
+        keep = ctx.enter_context(tc.tile_pool(name="keep", bufs=1))
+        psum = ctx.enter_context(tc.psum_pool(name="psum", bufs=1))
+        ctx.enter_context(tc.manual_schedule())
+
+        banks = [psum.tile([P, 4, P], F32, name="bank%d" % k) for k in range(8)]
+
+        w_raw = [[keep.tile([P, 2, D], BF16, name="w_raw%d%d" % (z, h)) for h in range(2)] for z in range(2)]
+        chunks = [(0, 1), (1, 1), (2, 1), (3, 1), (4, 2), (6, 2)] + [(f, 4) for f in range(8, FRAMES, 4)]
+        x_raw = [keep.tile([P, n, D], BF16, name="x_raw%d" % f0) for (f0, n) in chunks]
+        frame_src = {}
+        for k, (f0, n) in enumerate(chunks):
+            for i in range(n):
+                frame_src[f0 + i] = (k, i)
+
+        ident = keep.tile([P, P], F32, name="ident")
+        m16raw = keep.tile([P, 16], F32, name="m16raw")
+        m16 = keep.tile([P, 16], F32, name="m16")
+
+        w_grp = [keep.tile([P, 4, 2, P, 4], BF16, name="w_grp%d" % z, align_bytes=64) for z in range(2)]
+        w_codes = [keep.tile([P, 8 * P], U32, name="w_codes%d" % z, align_bytes=64) for z in range(2)]
+        w_scales = [keep.tile([P, 8 * P], U8, name="w_scales%d" % z, align_bytes=64) for z in range(2)]
+
+        x_grp = [keep.tile([P, 4, 2, P, 4], BF16, name="x_grp%d" % k, align_bytes=64) for k in range(2)]
+        x_codes = [keep.tile([P, 8 * P], U32, name="x_codes%d" % k, align_bytes=64) for k in range(2)]
+        x_scales = [keep.tile([P, 8 * P], U8, name="x_scales%d" % k, align_bytes=64) for k in range(2)]
+
+        h_grp = [keep.tile([P, 2, 2, P, 4], BF16, name="h_grp%d" % k, align_bytes=64) for k in range(3)]
+        ha_codes = [keep.tile([P, 4 * P], U32, name="ha_codes%d" % k, align_bytes=64) for k in range(HA)]
+        ha_scales = [keep.tile([P, 4 * P], U8, name="ha_scales%d" % k, align_bytes=64) for k in range(HA)]
+        hb_codes = [keep.tile([P, 16 * P], U32, name="hb_codes%d" % k, align_bytes=64) for k in range(2)]
+        hb_scales = [keep.tile([P, 16 * P], U8, name="hb_scales%d" % k, align_bytes=64) for k in range(2)]
+
+        sw_sb = [keep.tile([P, 4, P], F32, name="sw_sb%d" % k) for k in range(4)]
+        tw_tmp = [keep.tile([P, 64, 16], F32, name="tw_tmp%d" % k) for k in range(2)]
+        tw_res = keep.tile([P, B, 64], F32, name="tw_res")
+
+        xf = x.rearrange("b t j d -> j (b t) d")
+        swf = out_0.rearrange("b t j k -> j (b t) k")
+        w_dram = [w.rearrange("(p u) d -> p u d", u=4) for w in (Wtheta, Wphi)]
+
+        def load_w(z):
+            for h in range(2):
+                nc.sync.dma_start(out=w_raw[z][h][:], in_=w_dram[z][:, 2 * h:2 * h + 2, :])
+
+        def load_x(k):
+            f0, n = chunks[k]
+            nc.sync.dma_start(out=x_raw[k][:], in_=xf[:, f0:f0 + n, :])
+
+        load_w(0)
+        for k in range(4):
+            load_x(k)
+        load_w(1)
+        for k in range(4, len(chunks)):
+            load_x(k)
+
+        masks.make_identity(nc, ident[:])
+        for k in range(HA):
+            nc.vector.memset(ha_scales[k][:].bitcast(I32), 0)
+        nc.vector.tensor_reduce(out=m16raw[:], in_=ident[:].rearrange("p (t j) -> p j t", j=16), axis=AX.X, op=ALU.add)
+        nc.vector.tensor_scalar_mul(out=m16[:], in0=m16raw[:], scalar1=1.0 / T)
+
+        def cols(k, n=1):
+            return slice(k * P, (k + n) * P)
+
+        def transposes(bank, src):
+            words = src.bitcast(F32)
+            for c in range(2):
+                for h in range(2):
+                    nc.tensor.transpose(bank[:, 2 * c + h, :], words[:, 256 * c + h:256 * (c + 1):2], ident[:])
+
+        def copy_out(on_vector, dst, src):
+            if on_vector:
+                nc.vector.tensor_copy(out=dst, in_=src)
+            else:
+                nc.scalar.copy(out=dst, in_=src)
+
+        def evac_words(on_vector, grp, unit, bank):
+            copy_out(on_vector, grp[:].bitcast(F32)[:, unit], bank[:].rearrange("p (c h) r -> p c r h", h=2))
+
+        def quantise(codes, scales, grp, first, count):
+            flat = grp[:].rearrange("p a b r t -> p (a b r t)")
+            nc.vector.quantize_mx(out=codes[:, cols(first, count)].bitcast(FP8X4), scales=scales[:, cols(first, count)],
+                                  in_=flat[:, 4 * P * first:4 * P * (first + count)])
+
+        def w_transposes(z, ids):
+            for u in range(4):
+                transposes(banks[ids[u]], w_raw[z][u // 2][:, u % 2, :])
+
+        def x_transposes(f, bank):
+            k, i = frame_src[f]
+            transposes(bank, x_raw[k][:, i, :])
+
+        def stage1(f, z, bank, on_vector):
+            s = (f // 4) % 2
+            for u in range(4):
+                for c in range(2):
+                    nc.tensor.matmul_mx(
+                        out=bank[:, u, :],
+                        lhsT=w_codes[z][:, cols(2 * u + c)].bitcast(FP8X4),
+                        lhsT_scale=w_scales[z][:, cols(2 * u + c)],
+                        rhs=x_codes[s][:, cols(2 * (f % 4) + c)].bitcast(FP8X4),
+                        rhs_scale=x_scales[s][:, cols(2 * (f % 4) + c)],
+                        start=(c == 0),
+                        stop=(c == 1),
+                    )
+            copy_out(on_vector, h_grp[(f // 2) % 3][:, f % 2, z], bank[:].rearrange("p u r -> p r u"))
+
+        def h_quantise(pair, first=0, count=4):
+            quantise(ha_codes[pair % HA], ha_scales[pair % HA], h_grp[pair % 3], first, count)
+
+        def h_moves(pair, f0=0, nf=2):
+            b, t0 = pair // 4, 2 * (pair % 4) + f0
+            src = ha_codes[pair % HA][:].bitcast(I32).rearrange("p (f z a g c) -> p z g f a c", f=2, z=2, a=4, g=8)
+            dst = hb_codes[b % 2][:].bitcast(I32).rearrange("p (z g t a c) -> p z g t a c", z=2, g=8, t=T, a=4)
+            for z in range(2):
+                nc.vector.tensor_copy(out=dst[:, z, :, t0:t0 + nf], in_=src[:, z, :, f0:f0 + nf])
+            src = ha_scales[pair % HA][:].bitcast(I32).rearrange("p (f z a g) -> p z g f a", f=2, z=2, a=4)
+            dst = hb_scales[b % 2][:].bitcast(I32).rearrange("p (z g t a) -> p z g t a", z=2, g=8, t=T)
+            nc.vector.tensor_copy(out=dst[:, :, :, t0:t0 + nf], in_=src[:, :, :, f0:f0 + nf])
+
+        def sw_pass(f, bank):
+            s, fi = (f // 2) % HA, f % 2
+            nc.tensor.matmul_mx(
+                out=bank[:, f % 4, :],
+                lhsT=ha_codes[s][:, cols(2 * fi)].bitcast(FP8X4),
+                lhsT_scale=ha_scales[s][:, cols(2 * fi)],
+                rhs=ha_codes[s][:, cols(2 * fi + 1)].bitcast(FP8X4),
+                rhs_scale=ha_scales[s][:, cols(2 * fi + 1)],
+                start=True,
+                stop=True,
+            )
+
+        def sw_out(q, bank, queue):
+            nc.scalar.mul(out=sw_sb[q % 4][:], in_=bank[:], mul=1.0 / N)
+            queue.dma_start(out=swf[:, 4 * q:4 * q + 4, :], in_=sw_sb[q % 4][:])
+
+        def tw_passes(b, half, bank):
+            s = b % 2
+            for gg in range(4):
+                g = 4 * half + gg
+                nc.tensor.matmul_mx(
+                    out=bank[:, gg, :],
+                    lhsT=hb_codes[s][:, cols(g)].bitcast(FP8X4),
+                    lhsT_scale=hb_scales[s][:, cols(g)],
+                    rhs=hb_codes[s][:, cols(8 + g)].bitcast(FP8X4),
+                    rhs_scale=hb_scales[s][:, cols(8 + g)],
+                    start=True,
+                    stop=True,
+                )
+
+        def tw_mask(b, half, bank):
+            nc.vector.tensor_tensor(out=tw_tmp[b % 2][:, 32 * half:32 * half + 32, :],
+                                    in0=bank[:].rearrange("p g (s j) -> p (g s) j", j=16),
+                                    in1=m16[:].unsqueeze(1).to_broadcast([P, 32, 16]), op=ALU.mult)
+
+        def tw_out(b, queues):
+            nc.vector.tensor_reduce(out=tw_res[:, b, :], in_=tw_tmp[b % 2][:], axis=AX.X, op=ALU.add)
+            rows = out_1[b].rearrange("t (a g c) s -> c (t a) g s", a=4, g=8)
+            for c in range(4):
+                queues[c % len(queues)].dma_start(out=rows[c], in_=tw_res[c:P:4, b, :].rearrange("p (g s) -> p g s", s=T))
+
+        w_transposes(0, (0, 1, 2, 3))
+        for u in range(4):
+            evac_words(u % 2 == 0, w_grp[0], u, banks[u])
+            if u % 2 == 1:
+                quantise(w_codes[0], w_scales[0], w_grp[0], 4 * (u // 2), 4)
+        for f in range(4):
+            x_transposes(f, banks[4 + f])
+        for f in range(2):
+            evac_words(False, x_grp[0], f, banks[4 + f])
+            quantise(x_codes[0], x_scales[0], x_grp[0], 2 * f, 2)
+        evac_words(True, x_grp[0], 2, banks[6])
+        evac_words(False, x_grp[0], 3, banks[7])
+        quantise(x_codes[0], x_scales[0], x_grp[0], 4, 4)
+        stage1(0, 0, banks[0], False)
+        stage1(1, 0, banks[1], False)
+        w_transposes(1, (4, 5, 6, 7))
+        evac_words(True, w_grp[1], 0, banks[4])
+        evac_words(False, w_grp[1], 1, banks[5])
+        quantise(w_codes[1], w_scales[1], w_grp[1], 0, 4)
+        evac_words(False, w_grp[1], 2, banks[6])
+        evac_words(True, w_grp[1], 3, banks[7])
+        quantise(w_codes[1], w_scales[1], w_grp[1], 4, 4)
+        stage1(2, 0, banks[2], False)
+        stage1(3, 0, banks[3], False)
+        for f in range(4, 8):
+            x_transposes(f, banks[f - 4])
+        for f in range(4):
+            evac_words(f % 2 == 0, x_grp[1], f, banks[f])
+        quantise(x_codes[1], x_scales[1], x_grp[1], 0, 4)
+        quantise(x_codes[1], x_scales[1], x_grp[1], 4, 4)
+        for f in range(4):
+            stage1(f, 1, banks[4 + f], False)
+        h_quantise(0)
+        h_moves(0)
+
+        LASTQ = QUADS - 1
+        for J in range(1, QUADS):
+            nxt = J + 1
+            s = nxt % 2
+            more = nxt < QUADS
+            if more:
+                for i in range(4):
+                    x_transposes(4 * nxt + i, banks[i])
+                evac_words(True, x_grp[s], 0, banks[0])
+            h_quantise(2 * J - 1)
+            if more:
+                evac_words(True, x_grp[s], 1, banks[1])
+            h_moves(2 * J - 1)
+            if more:
+                evac_words(J % 2 == 1, x_grp[s], 2, banks[2])
+                evac_words(False, x_grp[s], 3, banks[3])
+                quantise(x_codes[s], x_scales[s], x_grp[s], 0, 4)
+                quantise(x_codes[s], x_scales[s], x_grp[s], 4, 4)
+            for k in range(4):
+                stage1(4 * J + k // 2, k % 2, banks[4 + k], False)
+            if J - 1 < QUADS - 1 - LATE:
+                for f in range(4 * J - 4, 4 * J):
+                    sw_pass(f, banks[0])
+                sw_out(J - 1, banks[0], nc.sync)
+            b = (J - 1) // 2
+            if (J - 1) % 2 == 1:
+                for half in range(2):
+                    tw_passes(b, half, banks[1 + half])
+                    tw_mask(b, half, banks[1 + half])
+            if J < LASTQ:
+                for k in range(4):
+                    stage1(4 * J + 2 + k // 2, k % 2, banks[4 + k], False)
+                h_quantise(2 * J)
+                if (J - 1) % 2 == 1:
+                    tw_out(b, [nc.sync])
+                h_moves(2 * J)
+            else:
+                h_quantise(2 * J)
+                h_moves(2 * J)
+                for fi in range(2):
+                    f = 4 * J + 2 + fi
+                    stage1(f, 0, banks[4 + 2 * fi], False)
+                    stage1(f, 1, banks[5 + 2 * fi], fi == 1)
+                    h_quantise(2 * J + 1, 2 * fi, 2)
+                for fi in range(2):
+                    h_moves(2 * J + 1, fi, 1)
+
+        for q in range(QUADS - 1 - LATE, QUADS - 1):
+            k = q - (QUADS - 1 - LATE)
+            for f in range(4 * q, 4 * q + 4):
+                sw_pass(f, banks[k])
+            sw_out(q, banks[k], nc.sync)
+        for f in range(FRAMES - 4, FRAMES):
+            sw_pass(f, banks[3])
+        for half in range(2):
+            tw_passes(B - 1, half, banks[4 + half])
+            tw_mask(B - 1, half, banks[4 + half])
+        sw_out(QUADS - 1, banks[3], nc.sync)
+        tw_out(B - 1, [nc.sync, nc.scalar])

@@ -56,6 +56,8 @@ def tile_higcin_volleyball_pa_t_kernel(tc, x, Wtheta, Wphi, out_0, out_1):
         hb_codes = [keep.tile([P, 16 * P], U32, name="hb_codes%d" % k, align_bytes=64) for k in range(2)]
         hb_scales = [keep.tile([P, 16 * P], U8, name="hb_scales%d" % k, align_bytes=64) for k in range(2)]
 
+        x_perm = [keep.tile([P, 4, D], BF16, name="x_perm%d" % k) for k in range(2)]
+
         sw_sb = [keep.tile([P, 4, P], F32, name="sw_sb%d" % k) for k in range(4)]
         tw_tmp = [keep.tile([P, 64, 16], F32, name="tw_tmp%d" % k) for k in range(2)]
         tw_res = keep.tile([P, B, 64], F32, name="tw_res")
@@ -107,6 +109,19 @@ def tile_higcin_volleyball_pa_t_kernel(tc, x, Wtheta, Wphi, out_0, out_1):
             flat = grp[:].rearrange("p a b r t -> p (a b r t)")
             nc.vector.quantize_mx(out=codes[:, cols(first, count)].bitcast(FP8X4), scales=scales[:, cols(first, count)],
                                   in_=flat[:, 4 * P * first:4 * P * (first + count)])
+
+        def permute_quad(q):
+            k, i = frame_src[4 * q]
+            for v in range(2):
+                src = x_raw[k][:, i + 2 * v:i + 2 * v + 2, :].rearrange("p f d -> p (f d)").bitcast(F32)
+                dst = x_perm[q % 2][:, 2 * v:2 * v + 2, :].rearrange("p f d -> p (f d)").bitcast(F32)
+                nc.vector.tensor_copy(out=dst.rearrange("p (c h w) -> p c h w", h=2, w=P),
+                                      in_=src.rearrange("p (c w h) -> p c h w", h=2, w=P))
+
+        def x_transposes_permuted(f, bank):
+            words = x_perm[(f // 4) % 2][:, f % 4, :].bitcast(F32)
+            for w in range(4):
+                nc.tensor.transpose(bank[:, w, :], words[:, cols(w)], ident[:])
 
         def w_transposes(z, ids):
             for u in range(4):
@@ -217,6 +232,7 @@ def tile_higcin_volleyball_pa_t_kernel(tc, x, Wtheta, Wphi, out_0, out_1):
         quantise(x_codes[1], x_scales[1], x_grp[1], 4, 4)
         for f in range(4):
             stage1(f, 1, banks[4 + f], False)
+        permute_quad(2)
         h_quantise(0)
         h_moves(0)
 
@@ -227,7 +243,7 @@ def tile_higcin_volleyball_pa_t_kernel(tc, x, Wtheta, Wphi, out_0, out_1):
             more = nxt < QUADS
             if more:
                 for i in range(4):
-                    x_transposes(4 * nxt + i, banks[i])
+                    x_transposes_permuted(4 * nxt + i, banks[i])
                 evac_words(True, x_grp[s], 0, banks[0])
             h_quantise(2 * J - 1)
             if more:
@@ -238,6 +254,8 @@ def tile_higcin_volleyball_pa_t_kernel(tc, x, Wtheta, Wphi, out_0, out_1):
                 evac_words(False, x_grp[s], 3, banks[3])
                 quantise(x_codes[s], x_scales[s], x_grp[s], 0, 4)
                 quantise(x_codes[s], x_scales[s], x_grp[s], 4, 4)
+            if J + 2 < QUADS:
+                permute_quad(J + 2)
             for k in range(4):
                 stage1(4 * J + k // 2, k % 2, banks[4 + k], False)
             if J - 1 < QUADS - 1 - LATE:

@@ -59,8 +59,9 @@ def tile_higcin_volleyball_pa_t_kernel(tc, x, Wtheta, Wphi, out_0, out_1):
         x_perm = [keep.tile([P, 4, D], BF16, name="x_perm%d" % k) for k in range(2)]
 
         sw_sb = [keep.tile([P, 4, P], F32, name="sw_sb%d" % k) for k in range(4)]
-        tw_tmp = [keep.tile([P, 64, 16], F32, name="tw_tmp%d" % k) for k in range(2)]
-        tw_res = keep.tile([P, B, 64], F32, name="tw_res")
+        tw_sb = [keep.tile([P, 16, 8, T], F32, name="tw_sb%d" % k) for k in range(2)]
+        tw_tmp = keep.tile([P, 64, 16], F32, name="tw_tmp")
+        tw_res = keep.tile([P, 64], F32, name="tw_res")
 
         xf = x.rearrange("b t j d -> j (b t) d")
         swf = out_0.rearrange("b t j k -> j (b t) k")
@@ -190,15 +191,24 @@ def tile_higcin_volleyball_pa_t_kernel(tc, x, Wtheta, Wphi, out_0, out_1):
                 )
 
         def tw_mask(b, half, bank):
-            nc.vector.tensor_tensor(out=tw_tmp[b % 2][:, 32 * half:32 * half + 32, :],
+            nc.vector.tensor_tensor(out=tw_tmp[:, 32 * half:32 * half + 32, :],
                                     in0=bank[:].rearrange("p g (s j) -> p (g s) j", j=16),
                                     in1=m16[:].unsqueeze(1).to_broadcast([P, 32, 16]), op=ALU.mult)
 
+        def tw_evac(b, half, bank):
+            nc.scalar.mul(out=tw_sb[b % 2][:, :, 4 * half:4 * half + 4, :],
+                          in_=bank[:].rearrange("p g (s n) -> p n g s", n=16), mul=1.0 / T)
+
+        def tw_store(b):
+            rows = out_1[b].rearrange("t (a g c) s -> a c t g s", a=4, g=8)
+            for n in range(16):
+                nc.sync.dma_start(out=rows[n // 4, n % 4], in_=tw_sb[b % 2][n:P:16, n, :, :])
+
         def tw_out(b, queues):
-            nc.vector.tensor_reduce(out=tw_res[:, b, :], in_=tw_tmp[b % 2][:], axis=AX.X, op=ALU.add)
+            nc.vector.tensor_reduce(out=tw_res[:], in_=tw_tmp[:], axis=AX.X, op=ALU.add)
             rows = out_1[b].rearrange("t (a g c) s -> c (t a) g s", a=4, g=8)
             for c in range(4):
-                queues[c % len(queues)].dma_start(out=rows[c], in_=tw_res[c:P:4, b, :].rearrange("p (g s) -> p g s", s=T))
+                queues[c % len(queues)].dma_start(out=rows[c], in_=tw_res[c:P:4, :].rearrange("p (g s) -> p g s", s=T))
 
         w_transposes(0, (0, 1, 2, 3))
         for u in range(4):
@@ -250,7 +260,7 @@ def tile_higcin_volleyball_pa_t_kernel(tc, x, Wtheta, Wphi, out_0, out_1):
                 evac_words(True, x_grp[s], 1, banks[1])
             h_moves(2 * J - 1)
             if more:
-                evac_words(J % 2 == 1, x_grp[s], 2, banks[2])
+                evac_words(True, x_grp[s], 2, banks[2])
                 evac_words(False, x_grp[s], 3, banks[3])
                 quantise(x_codes[s], x_scales[s], x_grp[s], 0, 4)
                 quantise(x_codes[s], x_scales[s], x_grp[s], 4, 4)
@@ -266,13 +276,12 @@ def tile_higcin_volleyball_pa_t_kernel(tc, x, Wtheta, Wphi, out_0, out_1):
             if (J - 1) % 2 == 1:
                 for half in range(2):
                     tw_passes(b, half, banks[1 + half])
-                    tw_mask(b, half, banks[1 + half])
+                    tw_evac(b, half, banks[1 + half])
+                tw_store(b)
             if J < LASTQ:
                 for k in range(4):
                     stage1(4 * J + 2 + k // 2, k % 2, banks[4 + k], False)
                 h_quantise(2 * J)
-                if (J - 1) % 2 == 1:
-                    tw_out(b, [nc.sync])
                 h_moves(2 * J)
             else:
                 h_quantise(2 * J)

@@ -252,21 +252,25 @@ def tile_higcin_volleyball_pa_t_kernel(tc, x, Wtheta, Wphi, out_0, out_1):
             s = nxt % 2
             more = nxt < QUADS
             if more:
-                for i in range(4):
+                for i in range(2):
                     x_transposes_permuted(4 * nxt + i, banks[i])
                 evac_words(True, x_grp[s], 0, banks[0])
             h_quantise(2 * J - 1)
             if more:
                 evac_words(True, x_grp[s], 1, banks[1])
             h_moves(2 * J - 1)
+            for k in range(2):
+                stage1(4 * J + k // 2, k % 2, banks[4 + k], False)
             if more:
+                for i in range(2, 4):
+                    x_transposes_permuted(4 * nxt + i, banks[i])
                 evac_words(True, x_grp[s], 2, banks[2])
                 evac_words(False, x_grp[s], 3, banks[3])
                 quantise(x_codes[s], x_scales[s], x_grp[s], 0, 4)
                 quantise(x_codes[s], x_scales[s], x_grp[s], 4, 4)
             if J + 2 < QUADS:
                 permute_quad(J + 2)
-            for k in range(4):
+            for k in range(2, 4):
                 stage1(4 * J + k // 2, k % 2, banks[4 + k], False)
             if J - 1 < QUADS - 1 - LATE:
                 for f in range(4 * J - 4, 4 * J):

@@ -16,7 +16,7 @@ P = 128
 B, T, N, D, L = 4, 8, 128, 1024, 512
 FRAMES = B * T
 QUADS = FRAMES // 4
-HA = 8
+HA = 4
 LATE = 3
 FLOPS = 2 * 2 * FRAMES * N * D * L + 2 * FRAMES * N * N * L + 2 * B * N * T * T * L
 
@@ -30,7 +30,8 @@ def tile_higcin_volleyball_pa_t_kernel(tc, x, Wtheta, Wphi, out_0, out_1):
 
         banks = [psum.tile([P, 4, P], F32, name="bank%d" % k) for k in range(8)]
 
-        w_raw = [[keep.tile([P, 2, D], BF16, name="w_raw%d%d" % (z, h)) for h in range(2)] for z in range(2)]
+        w_raw = [[keep.tile([P, D], BF16, name="w_raw%d%d" % (z, u)) for u in range(4)] for z in range(2)]
+        w_perm = [keep.tile([P, 4, D], BF16, name="w_perm%d" % z) for z in range(2)]
         chunks = [(0, 1), (1, 1), (2, 1), (3, 1), (4, 2), (6, 2)] + [(f, 4) for f in range(8, FRAMES, 4)]
         x_raw = [keep.tile([P, n, D], BF16, name="x_raw%d" % f0) for (f0, n) in chunks]
         frame_src = {}
@@ -51,8 +52,8 @@ def tile_higcin_volleyball_pa_t_kernel(tc, x, Wtheta, Wphi, out_0, out_1):
         x_scales = [keep.tile([P, 8 * P], U8, name="x_scales%d" % k, align_bytes=64) for k in range(2)]
 
         h_grp = [keep.tile([P, 2, 2, P, 4], BF16, name="h_grp%d" % k, align_bytes=64) for k in range(3)]
-        ha_codes = [keep.tile([P, 4 * P], U32, name="ha_codes%d" % k, align_bytes=64) for k in range(HA)]
-        ha_scales = [keep.tile([P, 4 * P], U8, name="ha_scales%d" % k, align_bytes=64) for k in range(HA)]
+        ha_codes = [keep.tile([P, 8 * P], U32, name="ha_codes%d" % k, align_bytes=64) for k in range(HA)]
+        ha_scales = [keep.tile([P, 8 * P], U8, name="ha_scales%d" % k, align_bytes=64) for k in range(HA)]
         hb_codes = [keep.tile([P, 16 * P], U32, name="hb_codes%d" % k, align_bytes=64) for k in range(2)]
         hb_scales = [keep.tile([P, 16 * P], U8, name="hb_scales%d" % k, align_bytes=64) for k in range(2)]
 
@@ -68,8 +69,8 @@ def tile_higcin_volleyball_pa_t_kernel(tc, x, Wtheta, Wphi, out_0, out_1):
         w_dram = [w.rearrange("(p u) d -> p u d", u=4) for w in (Wtheta, Wphi)]
 
         def load_w(z):
-            for h in range(2):
-                nc.sync.dma_start(out=w_raw[z][h][:], in_=w_dram[z][:, 2 * h:2 * h + 2, :])
+            for u in range(4):
+                nc.sync.dma_start(out=w_raw[z][u][:], in_=w_dram[z][:, u, :])
 
         def load_x(k):
             f0, n = chunks[k]
@@ -120,13 +121,27 @@ def tile_higcin_volleyball_pa_t_kernel(tc, x, Wtheta, Wphi, out_0, out_1):
                                       in_=src.rearrange("p (c w h) -> p c h w", h=2, w=P))
 
         def x_transposes_permuted(f, bank):
-            words = x_perm[(f // 4) % 2][:, f % 4, :].bitcast(F32)
+            transposes_permuted(bank, x_perm[(f // 4) % 2][:, f % 4, :])
+
+        def transposes_permuted(bank, src):
+            words = src.bitcast(F32)
             for w in range(4):
                 nc.tensor.transpose(bank[:, w, :], words[:, cols(w)], ident[:])
 
+        def permute(on_vector, dst, src):
+            copy_out(on_vector, dst.bitcast(F32).rearrange("p (c h w) -> p c h w", h=2, w=P),
+                     src.bitcast(F32).rearrange("p (c w h) -> p c h w", h=2, w=P))
+
+        def permute_frame(f, on_vector):
+            k, i = frame_src[f]
+            permute(on_vector, x_perm[(f // 4) % 2][:, f % 4, :], x_raw[k][:, i, :])
+
         def w_transposes(z, ids):
             for u in range(4):
-                transposes(banks[ids[u]], w_raw[z][u // 2][:, u % 2, :])
+                transposes_permuted(banks[ids[u]], w_perm[z][:, u, :])
+
+        def w_permute(z, u, on_vector):
+            permute(on_vector, w_perm[z][:, u, :], w_raw[z][u][:])
 
         def x_transposes(f, bank):
             k, i = frame_src[f]
@@ -148,20 +163,26 @@ def tile_higcin_volleyball_pa_t_kernel(tc, x, Wtheta, Wphi, out_0, out_1):
             copy_out(on_vector, h_grp[(f // 2) % 3][:, f % 2, z], bank[:].rearrange("p u r -> p r u"))
 
         def h_quantise(pair, first=0, count=4):
-            quantise(ha_codes[pair % HA], ha_scales[pair % HA], h_grp[pair % 3], first, count)
+            q, at = pair // 2, 4 * (pair % 2)
+            flat = h_grp[pair % 3][:].rearrange("p a b r t -> p (a b r t)")
+            nc.vector.quantize_mx(out=ha_codes[q % HA][:, cols(at + first, count)].bitcast(FP8X4),
+                                  scales=ha_scales[q % HA][:, cols(at + first, count)],
+                                  in_=flat[:, 4 * P * first:4 * P * (first + count)])
 
-        def h_moves(pair, f0=0, nf=2):
-            b, t0 = pair // 4, 2 * (pair % 4) + f0
-            src = ha_codes[pair % HA][:].bitcast(I32).rearrange("p (f z a g c) -> p z g f a c", f=2, z=2, a=4, g=8)
+        def code_moves(z, q, f0=0, nf=4):
+            b, t0 = q // 2, 4 * (q % 2) + f0
+            src = ha_codes[q % HA][:].bitcast(I32).rearrange("p (f z a g c) -> p z g f a c", f=4, z=2, a=4, g=8)
             dst = hb_codes[b % 2][:].bitcast(I32).rearrange("p (z g t a c) -> p z g t a c", z=2, g=8, t=T, a=4)
-            for z in range(2):
-                nc.vector.tensor_copy(out=dst[:, z, :, t0:t0 + nf], in_=src[:, z, :, f0:f0 + nf])
-            src = ha_scales[pair % HA][:].bitcast(I32).rearrange("p (f z a g) -> p z g f a", f=2, z=2, a=4)
+            nc.vector.tensor_copy(out=dst[:, z, :, t0:t0 + nf], in_=src[:, z, :, f0:f0 + nf])
+
+        def scale_moves(q, f0=0, nf=4):
+            b, t0 = q // 2, 4 * (q % 2) + f0
+            src = ha_scales[q % HA][:].bitcast(I32).rearrange("p (f z a g) -> p z g f a", f=4, z=2, a=4)
             dst = hb_scales[b % 2][:].bitcast(I32).rearrange("p (z g t a) -> p z g t a", z=2, g=8, t=T)
             nc.vector.tensor_copy(out=dst[:, :, :, t0:t0 + nf], in_=src[:, :, :, f0:f0 + nf])
 
         def sw_pass(f, bank):
-            s, fi = (f // 2) % HA, f % 2
+            s, fi = (f // 4) % HA, f % 4
             nc.tensor.matmul_mx(
                 out=bank[:, f % 4, :],
                 lhsT=ha_codes[s][:, cols(2 * fi)].bitcast(FP8X4),
@@ -172,9 +193,9 @@ def tile_higcin_volleyball_pa_t_kernel(tc, x, Wtheta, Wphi, out_0, out_1):
                 stop=True,
             )
 
-        def sw_out(q, bank, queue):
-            nc.scalar.mul(out=sw_sb[q % 4][:], in_=bank[:], mul=1.0 / N)
-            queue.dma_start(out=swf[:, 4 * q:4 * q + 4, :], in_=sw_sb[q % 4][:])
+        def sw_out(q, bank, g0, n):
+            nc.scalar.mul(out=sw_sb[q % 4][:, g0:g0 + n], in_=bank[:, g0:g0 + n], mul=1.0 / N)
+            nc.sync.dma_start(out=swf[:, 4 * q + g0:4 * q + g0 + n, :], in_=sw_sb[q % 4][:, g0:g0 + n])
 
         def tw_passes(b, half, bank):
             s = b % 2
@@ -204,70 +225,83 @@ def tile_higcin_volleyball_pa_t_kernel(tc, x, Wtheta, Wphi, out_0, out_1):
             for n in range(16):
                 nc.sync.dma_start(out=rows[n // 4, n % 4], in_=tw_sb[b % 2][n:P:16, n, :, :])
 
-        def tw_out(b, queues):
+        def tw_out(b):
             nc.vector.tensor_reduce(out=tw_res[:], in_=tw_tmp[:], axis=AX.X, op=ALU.add)
             rows = out_1[b].rearrange("t (a g c) s -> c (t a) g s", a=4, g=8)
             for c in range(4):
-                queues[c % len(queues)].dma_start(out=rows[c], in_=tw_res[c:P:4, :].rearrange("p (g s) -> p g s", s=T))
+                queue = nc.sync if c % 2 == 0 else nc.scalar
+                queue.dma_start(out=rows[c], in_=tw_res[c:P:4, :].rearrange("p (g s) -> p g s", s=T))
 
-        w_transposes(0, (0, 1, 2, 3))
         for u in range(4):
-            evac_words(u % 2 == 0, w_grp[0], u, banks[u])
-            if u % 2 == 1:
-                quantise(w_codes[0], w_scales[0], w_grp[0], 4 * (u // 2), 4)
+            w_permute(0, u, True)
+        w_transposes(0, (0, 1, 2, 3))
+        evac_words(False, w_grp[0], 0, banks[0])
+        evac_words(True, w_grp[0], 1, banks[1])
+        evac_words(False, w_grp[0], 2, banks[2])
+        quantise(w_codes[0], w_scales[0], w_grp[0], 0, 4)
+        evac_words(False, w_grp[0], 3, banks[3])
         for f in range(4):
             x_transposes(f, banks[4 + f])
-        for f in range(2):
-            evac_words(False, x_grp[0], f, banks[4 + f])
-            quantise(x_codes[0], x_scales[0], x_grp[0], 2 * f, 2)
-        evac_words(True, x_grp[0], 2, banks[6])
-        evac_words(False, x_grp[0], 3, banks[7])
+        evac_words(True, x_grp[0], 0, banks[4])
+        quantise(w_codes[0], w_scales[0], w_grp[0], 4, 4)
+        quantise(x_codes[0], x_scales[0], x_grp[0], 0, 2)
+        evac_words(False, x_grp[0], 1, banks[5])
+        evac_words(False, x_grp[0], 2, banks[6])
+        w_permute(1, 0, False)
+        quantise(x_codes[0], x_scales[0], x_grp[0], 2, 2)
+        evac_words(True, x_grp[0], 3, banks[7])
+        w_permute(1, 1, False)
+        w_permute(1, 2, True)
+        w_permute(1, 3, True)
         quantise(x_codes[0], x_scales[0], x_grp[0], 4, 4)
+        permute_frame(4, True)
+        permute_frame(5, True)
         stage1(0, 0, banks[0], False)
         stage1(1, 0, banks[1], False)
         w_transposes(1, (4, 5, 6, 7))
         evac_words(True, w_grp[1], 0, banks[4])
         evac_words(False, w_grp[1], 1, banks[5])
+        evac_words(True, w_grp[1], 2, banks[6])
+        evac_words(False, w_grp[1], 3, banks[7])
         quantise(w_codes[1], w_scales[1], w_grp[1], 0, 4)
-        evac_words(False, w_grp[1], 2, banks[6])
-        evac_words(True, w_grp[1], 3, banks[7])
-        quantise(w_codes[1], w_scales[1], w_grp[1], 4, 4)
         stage1(2, 0, banks[2], False)
         stage1(3, 0, banks[3], False)
-        for f in range(4, 8):
+        quantise(w_codes[1], w_scales[1], w_grp[1], 4, 4)
+        for f in range(4, 6):
+            x_transposes_permuted(f, banks[f - 4])
+        for f in range(6, 8):
             x_transposes(f, banks[f - 4])
-        for f in range(4):
-            evac_words(f % 2 == 0, x_grp[1], f, banks[f])
+        evac_words(True, x_grp[1], 0, banks[0])
+        evac_words(False, x_grp[1], 1, banks[1])
+        evac_words(True, x_grp[1], 2, banks[2])
         quantise(x_codes[1], x_scales[1], x_grp[1], 0, 4)
-        quantise(x_codes[1], x_scales[1], x_grp[1], 4, 4)
+        evac_words(False, x_grp[1], 3, banks[3])
         for f in range(4):
             stage1(f, 1, banks[4 + f], False)
         permute_quad(2)
+        quantise(x_codes[1], x_scales[1], x_grp[1], 4, 4)
         h_quantise(0)
-        h_moves(0)
 
         LASTQ = QUADS - 1
-        for J in range(1, QUADS):
+        for J in range(1, LASTQ):
             nxt = J + 1
             s = nxt % 2
-            more = nxt < QUADS
-            if more:
-                for i in range(2):
-                    x_transposes_permuted(4 * nxt + i, banks[i])
-                evac_words(True, x_grp[s], 0, banks[0])
+            for i in range(2):
+                x_transposes_permuted(4 * nxt + i, banks[i])
+            evac_words(True, x_grp[s], 0, banks[0])
             h_quantise(2 * J - 1)
-            if more:
-                evac_words(True, x_grp[s], 1, banks[1])
-            h_moves(2 * J - 1)
+            evac_words(True, x_grp[s], 1, banks[1])
+            code_moves(0, J - 1)
             for k in range(2):
                 stage1(4 * J + k // 2, k % 2, banks[4 + k], False)
-            if more:
-                for i in range(2, 4):
-                    x_transposes_permuted(4 * nxt + i, banks[i])
-                evac_words(True, x_grp[s], 2, banks[2])
-                evac_words(False, x_grp[s], 3, banks[3])
-                quantise(x_codes[s], x_scales[s], x_grp[s], 0, 4)
-                quantise(x_codes[s], x_scales[s], x_grp[s], 4, 4)
+            for i in range(2, 4):
+                x_transposes_permuted(4 * nxt + i, banks[i])
+            evac_words(False, x_grp[s], 2, banks[2])
+            evac_words(J % 2 == 0, x_grp[s], 3, banks[3])
+            code_moves(1, J - 1)
+            quantise(x_codes[s], x_scales[s], x_grp[s], 0, 4)
+            scale_moves(J - 1)
+            quantise(x_codes[s], x_scales[s], x_grp[s], 4, 4)
             if J + 2 < QUADS:
                 permute_quad(J + 2)
             for k in range(2, 4):
@@ -275,38 +309,57 @@ def tile_higcin_volleyball_pa_t_kernel(tc, x, Wtheta, Wphi, out_0, out_1):
             if J - 1 < QUADS - 1 - LATE:
                 for f in range(4 * J - 4, 4 * J):
                     sw_pass(f, banks[0])
-                sw_out(J - 1, banks[0], nc.sync)
-            b = (J - 1) // 2
+                sw_out(J - 1, banks[0], 0, 4)
+            helps = J == LASTQ - 1
+            for k in range(2):
+                stage1(4 * J + 2, k, banks[4 + k], helps and k == 1)
             if (J - 1) % 2 == 1:
+                b = (J - 1) // 2
                 for half in range(2):
                     tw_passes(b, half, banks[1 + half])
                     tw_evac(b, half, banks[1 + half])
                 tw_store(b)
-            if J < LASTQ:
-                for k in range(4):
-                    stage1(4 * J + 2 + k // 2, k % 2, banks[4 + k], False)
-                h_quantise(2 * J)
-                h_moves(2 * J)
-            else:
-                h_quantise(2 * J)
-                h_moves(2 * J)
-                for fi in range(2):
-                    f = 4 * J + 2 + fi
-                    stage1(f, 0, banks[4 + 2 * fi], False)
-                    stage1(f, 1, banks[5 + 2 * fi], fi == 1)
-                    h_quantise(2 * J + 1, 2 * fi, 2)
-                for fi in range(2):
-                    h_moves(2 * J + 1, fi, 1)
+            h_quantise(2 * J)
+            for k in range(2):
+                stage1(4 * J + 3, k, banks[6 + k], helps and k == 1)
 
-        for q in range(QUADS - 1 - LATE, QUADS - 1):
+        f0 = FRAMES - 4
+        stage1(f0, 0, banks[4], False)
+        stage1(f0, 1, banks[5], False)
+        stage1(f0 + 1, 0, banks[6], False)
+        h_quantise(2 * LASTQ - 1)
+        code_moves(0, LASTQ - 1)
+        stage1(f0 + 1, 1, banks[7], True)
+        code_moves(1, LASTQ - 1)
+        stage1(f0 + 2, 0, banks[0], False)
+        stage1(f0 + 2, 1, banks[1], False)
+        h_quantise(2 * LASTQ)
+        stage1(f0 + 3, 0, banks[2], False)
+        scale_moves(LASTQ - 1)
+        code_moves(0, LASTQ, 0, 2)
+        code_moves(1, LASTQ, 0, 2)
+        scale_moves(LASTQ, 0, 2)
+        h_quantise(2 * LASTQ + 1, 0, 2)
+        stage1(f0 + 3, 1, banks[3], True)
+        code_moves(0, LASTQ, 2, 1)
+        code_moves(1, LASTQ, 2, 1)
+        scale_moves(LASTQ, 2, 1)
+        h_quantise(2 * LASTQ + 1, 2, 2)
+        code_moves(0, LASTQ, 3, 1)
+        code_moves(1, LASTQ, 3, 1)
+        scale_moves(LASTQ, 3, 1)
+        for q in range(QUADS - 1 - LATE, LASTQ):
             k = q - (QUADS - 1 - LATE)
             for f in range(4 * q, 4 * q + 4):
-                sw_pass(f, banks[k])
-            sw_out(q, banks[k], nc.sync)
-        for f in range(FRAMES - 4, FRAMES):
-            sw_pass(f, banks[3])
+                sw_pass(f, banks[4 + k])
+            sw_out(q, banks[4 + k], 0, 4)
+        for f in range(f0, f0 + 3):
+            sw_pass(f, banks[7])
+        for f in range(f0 + 3, FRAMES):
+            sw_pass(f, banks[7])
         for half in range(2):
-            tw_passes(B - 1, half, banks[4 + half])
-            tw_mask(B - 1, half, banks[4 + half])
-        sw_out(QUADS - 1, banks[3], nc.sync)
-        tw_out(B - 1, [nc.sync, nc.scalar])
+            tw_passes(B - 1, half, banks[half])
+        for half in range(2):
+            tw_mask(B - 1, half, banks[half])
+        sw_out(LASTQ, banks[7], 0, 4)
+        tw_out(B - 1)

@@ -9,15 +9,13 @@ U32 = mybir.dt.uint32
 I32 = mybir.dt.int32
 U8 = mybir.dt.uint8
 FP8X4 = mybir.dt.float8_e4m3fn_x4
-ALU = mybir.AluOpType
-AX = mybir.AxisListType
 
 P = 128
 B, T, N, D, L = 4, 8, 128, 1024, 512
 FRAMES = B * T
 QUADS = FRAMES // 4
 HA = 4
-LATE = 3
+LATE = 2
 FLOPS = 2 * 2 * FRAMES * N * D * L + 2 * FRAMES * N * N * L + 2 * B * N * T * T * L
 
 
@@ -31,7 +29,7 @@ def tile_higcin_volleyball_pa_t_kernel(tc, x, Wtheta, Wphi, out_0, out_1):
         banks = [psum.tile([P, 4, P], F32, name="bank%d" % k) for k in range(8)]
 
         w_raw = [[keep.tile([P, D], BF16, name="w_raw%d%d" % (z, u)) for u in range(4)] for z in range(2)]
-        w_perm = [keep.tile([P, 4, D], BF16, name="w_perm%d" % z) for z in range(2)]
+        w_perm = keep.tile([P, 4, D], BF16, name="w_perm")
         chunks = [(0, 1), (1, 1), (2, 1), (3, 1), (4, 2), (6, 2)] + [(f, 4) for f in range(8, FRAMES, 4)]
         x_raw = [keep.tile([P, n, D], BF16, name="x_raw%d" % f0) for (f0, n) in chunks]
         frame_src = {}
@@ -40,8 +38,6 @@ def tile_higcin_volleyball_pa_t_kernel(tc, x, Wtheta, Wphi, out_0, out_1):
                 frame_src[f0 + i] = (k, i)
 
         ident = keep.tile([P, P], F32, name="ident")
-        m16raw = keep.tile([P, 16], F32, name="m16raw")
-        m16 = keep.tile([P, 16], F32, name="m16")
 
         w_grp = [keep.tile([P, 4, 2, P, 4], BF16, name="w_grp%d" % z, align_bytes=64) for z in range(2)]
         w_codes = [keep.tile([P, 8 * P], U32, name="w_codes%d" % z, align_bytes=64) for z in range(2)]
@@ -61,11 +57,9 @@ def tile_higcin_volleyball_pa_t_kernel(tc, x, Wtheta, Wphi, out_0, out_1):
 
         sw_sb = [keep.tile([P, 4, P], F32, name="sw_sb%d" % k) for k in range(4)]
         tw_sb = [keep.tile([P, 16, 8, T], F32, name="tw_sb%d" % k) for k in range(2)]
-        tw_tmp = keep.tile([P, 64, 16], F32, name="tw_tmp")
-        tw_res = keep.tile([P, 64], F32, name="tw_res")
+        tw_last = keep.tile([P, 4, 8, T], F32, name="tw_last")
 
         xf = x.rearrange("b t j d -> j (b t) d")
-        swf = out_0.rearrange("b t j k -> j (b t) k")
         w_dram = [w.rearrange("(p u) d -> p u d", u=4) for w in (Wtheta, Wphi)]
 
         def load_w(z):
@@ -86,8 +80,6 @@ def tile_higcin_volleyball_pa_t_kernel(tc, x, Wtheta, Wphi, out_0, out_1):
         masks.make_identity(nc, ident[:])
         for k in range(HA):
             nc.vector.memset(ha_scales[k][:].bitcast(I32), 0)
-        nc.vector.tensor_reduce(out=m16raw[:], in_=ident[:].rearrange("p (t j) -> p j t", j=16), axis=AX.X, op=ALU.add)
-        nc.vector.tensor_scalar_mul(out=m16[:], in0=m16raw[:], scalar1=1.0 / T)
 
         def cols(k, n=1):
             return slice(k * P, (k + n) * P)
@@ -115,10 +107,8 @@ def tile_higcin_volleyball_pa_t_kernel(tc, x, Wtheta, Wphi, out_0, out_1):
         def permute_quad(q):
             k, i = frame_src[4 * q]
             for v in range(2):
-                src = x_raw[k][:, i + 2 * v:i + 2 * v + 2, :].rearrange("p f d -> p (f d)").bitcast(F32)
-                dst = x_perm[q % 2][:, 2 * v:2 * v + 2, :].rearrange("p f d -> p (f d)").bitcast(F32)
-                nc.vector.tensor_copy(out=dst.rearrange("p (c h w) -> p c h w", h=2, w=P),
-                                      in_=src.rearrange("p (c w h) -> p c h w", h=2, w=P))
+                permute(True, x_perm[q % 2][:, 2 * v:2 * v + 2, :].rearrange("p f d -> p (f d)"),
+                        x_raw[k][:, i + 2 * v:i + 2 * v + 2, :].rearrange("p f d -> p (f d)"))
 
         def x_transposes_permuted(f, bank):
             transposes_permuted(bank, x_perm[(f // 4) % 2][:, f % 4, :])
@@ -138,10 +128,13 @@ def tile_higcin_volleyball_pa_t_kernel(tc, x, Wtheta, Wphi, out_0, out_1):
 
         def w_transposes(z, ids):
             for u in range(4):
-                transposes_permuted(banks[ids[u]], w_perm[z][:, u, :])
+                if z == 0:
+                    transposes(banks[ids[u]], w_raw[0][u][:])
+                else:
+                    transposes_permuted(banks[ids[u]], w_perm[:, u, :])
 
-        def w_permute(z, u, on_vector):
-            permute(on_vector, w_perm[z][:, u, :], w_raw[z][u][:])
+        def w_permute(u, on_vector):
+            permute(on_vector, w_perm[:, u, :], w_raw[1][u][:])
 
         def x_transposes(f, bank):
             k, i = frame_src[f]
@@ -160,7 +153,8 @@ def tile_higcin_volleyball_pa_t_kernel(tc, x, Wtheta, Wphi, out_0, out_1):
                         start=(c == 0),
                         stop=(c == 1),
                     )
-            copy_out(on_vector, h_grp[(f // 2) % 3][:, f % 2, z], bank[:].rearrange("p u r -> p r u"))
+            copy_out(on_vector, h_grp[(f // 2) % 3][:, f % 2, z].rearrange("p (m c) u -> p m c u", c=4),
+                     bank[:].rearrange("p u (c m) -> p m c u", c=4))
 
         def h_quantise(pair, first=0, count=4):
             q, at = pair // 2, 4 * (pair % 2)
@@ -169,17 +163,28 @@ def tile_higcin_volleyball_pa_t_kernel(tc, x, Wtheta, Wphi, out_0, out_1):
                                   scales=ha_scales[q % HA][:, cols(at + first, count)],
                                   in_=flat[:, 4 * P * first:4 * P * (first + count)])
 
+        def moves(src, dst, q, f0, nf):
+            t0 = 4 * (q % 2) + f0
+            nc.vector.tensor_copy(out=dst[:, :, :, t0:t0 + nf], in_=src[:, :, :, f0:f0 + nf])
+
         def code_moves(z, q, f0=0, nf=4):
-            b, t0 = q // 2, 4 * (q % 2) + f0
-            src = ha_codes[q % HA][:].bitcast(I32).rearrange("p (f z a g c) -> p z g f a c", f=4, z=2, a=4, g=8)
-            dst = hb_codes[b % 2][:].bitcast(I32).rearrange("p (z g t a c) -> p z g t a c", z=2, g=8, t=T, a=4)
-            nc.vector.tensor_copy(out=dst[:, z, :, t0:t0 + nf], in_=src[:, z, :, f0:f0 + nf])
+            words = hb_codes[(q // 2) % 2][:, cols(8 * z, 8)].bitcast(I32)
+            src = ha_codes[q % HA][:].bitcast(I32).rearrange("p (f z a g c) -> p z g a f c", f=4, z=2, a=4, g=8)[:, z]
+            if z == 0:
+                dst = words.rearrange("p (g a t c) -> p g a t c", g=8, t=T, a=4)
+            else:
+                dst = words.rearrange("p (g t a c) -> p g a t c", g=8, t=T, a=4)
+            moves(src, dst, q, f0, nf)
 
         def scale_moves(q, f0=0, nf=4):
-            b, t0 = q // 2, 4 * (q % 2) + f0
-            src = ha_scales[q % HA][:].bitcast(I32).rearrange("p (f z a g) -> p z g f a", f=4, z=2, a=4)
-            dst = hb_scales[b % 2][:].bitcast(I32).rearrange("p (z g t a) -> p z g t a", z=2, g=8, t=T)
-            nc.vector.tensor_copy(out=dst[:, :, :, t0:t0 + nf], in_=src[:, :, :, f0:f0 + nf])
+            for z in range(2):
+                words = hb_scales[(q // 2) % 2][:, cols(8 * z, 8)].bitcast(I32)
+                src = ha_scales[q % HA][:].bitcast(I32).rearrange("p (f z a g) -> p z g a f", f=4, z=2, a=4)[:, z]
+                if z == 0:
+                    dst = words.rearrange("p (g a t) -> p g a t", g=8, t=T)
+                else:
+                    dst = words.rearrange("p (g t a) -> p g a t", g=8, t=T)
+                moves(src, dst, q, f0, nf)
 
         def sw_pass(f, bank):
             s, fi = (f // 4) % HA, f % 4
@@ -194,8 +199,10 @@ def tile_higcin_volleyball_pa_t_kernel(tc, x, Wtheta, Wphi, out_0, out_1):
             )
 
         def sw_out(q, bank, g0, n):
-            nc.scalar.mul(out=sw_sb[q % 4][:, g0:g0 + n], in_=bank[:, g0:g0 + n], mul=1.0 / N)
-            nc.sync.dma_start(out=swf[:, 4 * q + g0:4 * q + g0 + n, :], in_=sw_sb[q % 4][:, g0:g0 + n])
+            nc.scalar.mul(out=sw_sb[q % 4][:, g0:g0 + n].rearrange("p f (c m) -> p f c m", c=4),
+                          in_=bank[:, g0:g0 + n].rearrange("p f (m c) -> p f c m", c=4), mul=1.0 / N)
+            for f in range(4 * q + g0, 4 * q + g0 + n):
+                nc.sync.dma_start(out=out_0[f // T, f % T].rearrange("(c m) k -> m c k", c=4), in_=sw_sb[q % 4][:, f % 4, :])
 
         def tw_passes(b, half, bank):
             s = b % 2
@@ -211,48 +218,50 @@ def tile_higcin_volleyball_pa_t_kernel(tc, x, Wtheta, Wphi, out_0, out_1):
                     stop=True,
                 )
 
-        def tw_mask(b, half, bank):
-            nc.vector.tensor_tensor(out=tw_tmp[:, 32 * half:32 * half + 32, :],
-                                    in0=bank[:].rearrange("p g (s j) -> p (g s) j", j=16),
-                                    in1=m16[:].unsqueeze(1).to_broadcast([P, 32, 16]), op=ALU.mult)
-
         def tw_evac(b, half, bank):
             nc.scalar.mul(out=tw_sb[b % 2][:, :, 4 * half:4 * half + 4, :],
                           in_=bank[:].rearrange("p g (s n) -> p n g s", n=16), mul=1.0 / T)
 
         def tw_store(b):
-            rows = out_1[b].rearrange("t (a g c) s -> a c t g s", a=4, g=8)
-            for n in range(16):
-                nc.sync.dma_start(out=rows[n // 4, n % 4], in_=tw_sb[b % 2][n:P:16, n, :, :])
+            rows = out_1[b].rearrange("t (c a g) s -> a c t (g s)", c=4, a=4)
+            for a in range(4):
+                for c in range(4):
+                    nc.sync.dma_start(out=rows[a, c], in_=tw_sb[b % 2][32 * a + c:32 * a + 32:4, 4 * a + c].rearrange("p g s -> p (g s)"))
 
-        def tw_out(b):
-            nc.vector.tensor_reduce(out=tw_res[:], in_=tw_tmp[:], axis=AX.X, op=ALU.add)
-            rows = out_1[b].rearrange("t (a g c) s -> c (t a) g s", a=4, g=8)
+        def tw_evac_last(half, bank, on_vector):
+            for a in range(4):
+                q = slice(32 * a, 32 * a + 32)
+                dst = tw_last[q, :, 4 * half:4 * half + 4, :]
+                src = bank[q].rearrange("p g (s a c) -> p a c g s", a=4, c=4)[:, a]
+                if on_vector:
+                    nc.vector.tensor_scalar_mul(out=dst, in0=src, scalar1=1.0 / T)
+                else:
+                    nc.scalar.mul(out=dst, in_=src, mul=1.0 / T)
+
+        def tw_store_last(b):
+            rows = out_1[b].rearrange("t (c a g) s -> c a t (g s)", c=4, a=4)
             for c in range(4):
-                queue = nc.sync if c % 2 == 0 else nc.scalar
-                queue.dma_start(out=rows[c], in_=tw_res[c:P:4, :].rearrange("p (g s) -> p g s", s=T))
+                nc.sync.dma_start(out=rows[c], in_=tw_last[c:P:4, c].rearrange("p g s -> p (g s)"))
 
-        for u in range(4):
-            w_permute(0, u, True)
         w_transposes(0, (0, 1, 2, 3))
         evac_words(False, w_grp[0], 0, banks[0])
         evac_words(True, w_grp[0], 1, banks[1])
         evac_words(False, w_grp[0], 2, banks[2])
         quantise(w_codes[0], w_scales[0], w_grp[0], 0, 4)
-        evac_words(False, w_grp[0], 3, banks[3])
+        evac_words(True, w_grp[0], 3, banks[3])
         for f in range(4):
             x_transposes(f, banks[4 + f])
-        evac_words(True, x_grp[0], 0, banks[4])
+        evac_words(False, x_grp[0], 0, banks[4])
         quantise(w_codes[0], w_scales[0], w_grp[0], 4, 4)
         quantise(x_codes[0], x_scales[0], x_grp[0], 0, 2)
         evac_words(False, x_grp[0], 1, banks[5])
         evac_words(False, x_grp[0], 2, banks[6])
-        w_permute(1, 0, False)
+        w_permute(0, False)
         quantise(x_codes[0], x_scales[0], x_grp[0], 2, 2)
         evac_words(True, x_grp[0], 3, banks[7])
-        w_permute(1, 1, False)
-        w_permute(1, 2, True)
-        w_permute(1, 3, True)
+        w_permute(1, False)
+        w_permute(2, True)
+        w_permute(3, True)
         quantise(x_codes[0], x_scales[0], x_grp[0], 4, 4)
         permute_frame(4, True)
         permute_frame(5, True)
@@ -299,11 +308,11 @@ def tile_higcin_volleyball_pa_t_kernel(tc, x, Wtheta, Wphi, out_0, out_1):
             evac_words(False, x_grp[s], 2, banks[2])
             evac_words(J % 2 == 0, x_grp[s], 3, banks[3])
             code_moves(1, J - 1)
-            quantise(x_codes[s], x_scales[s], x_grp[s], 0, 4)
             scale_moves(J - 1)
-            quantise(x_codes[s], x_scales[s], x_grp[s], 4, 4)
             if J + 2 < QUADS:
                 permute_quad(J + 2)
+            quantise(x_codes[s], x_scales[s], x_grp[s], 0, 4)
+            quantise(x_codes[s], x_scales[s], x_grp[s], 4, 4)
             for k in range(2, 4):
                 stage1(4 * J + k // 2, k % 2, banks[4 + k], False)
             if J - 1 < QUADS - 1 - LATE:
@@ -359,7 +368,7 @@ def tile_higcin_volleyball_pa_t_kernel(tc, x, Wtheta, Wphi, out_0, out_1):
             sw_pass(f, banks[7])
         for half in range(2):
             tw_passes(B - 1, half, banks[half])
-        for half in range(2):
-            tw_mask(B - 1, half, banks[half])
         sw_out(LASTQ, banks[7], 0, 4)
-        tw_out(B - 1)
+        for half in range(2):
+            tw_evac_last(half, banks[half], half == 0)
+        tw_store_last(B - 1)

@@ -126,12 +126,11 @@ def tile_higcin_volleyball_pa_t_kernel(tc, x, Wtheta, Wphi, out_0, out_1):
             k, i = frame_src[f]
             permute(on_vector, x_perm[(f // 4) % 2][:, f % 4, :], x_raw[k][:, i, :])
 
-        def w_transposes(z, ids):
-            for u in range(4):
-                if z == 0:
-                    transposes(banks[ids[u]], w_raw[0][u][:])
-                else:
-                    transposes_permuted(banks[ids[u]], w_perm[:, u, :])
+        def w_transposes(z, u, bank):
+            if z == 0:
+                transposes(bank, w_raw[0][u][:])
+            else:
+                transposes_permuted(bank, w_perm[:, u, :])
 
         def w_permute(u, on_vector):
             permute(on_vector, w_perm[:, u, :], w_raw[1][u][:])
@@ -153,8 +152,11 @@ def tile_higcin_volleyball_pa_t_kernel(tc, x, Wtheta, Wphi, out_0, out_1):
                         start=(c == 0),
                         stop=(c == 1),
                     )
-            copy_out(on_vector, h_grp[(f // 2) % 3][:, f % 2, z].rearrange("p (m c) u -> p m c u", c=4),
-                     bank[:].rearrange("p u (c m) -> p m c u", c=4))
+            dst = h_grp[(f // 2) % 3][:, f % 2, z]
+            if f // T < B - 1:
+                copy_out(on_vector, dst, bank[:].rearrange("p u n -> p n u"))
+            else:
+                copy_out(on_vector, dst.rearrange("p (m c) u -> p m c u", c=4), bank[:].rearrange("p u (c m) -> p m c u", c=4))
 
         def h_quantise(pair, first=0, count=4):
             q, at = pair // 2, 4 * (pair % 2)
@@ -167,6 +169,13 @@ def tile_higcin_volleyball_pa_t_kernel(tc, x, Wtheta, Wphi, out_0, out_1):
             t0 = 4 * (q % 2) + f0
             nc.vector.tensor_copy(out=dst[:, :, :, t0:t0 + nf], in_=src[:, :, :, f0:f0 + nf])
 
+        def quad_moves(q):
+            b, t0 = (q // 2) % 2, 4 * (q % 2)
+            for (src, dst, n) in ((ha_codes[q % HA], hb_codes[b], 16), (ha_scales[q % HA], hb_scales[b], 4)):
+                words = dst[:].bitcast(I32).rearrange("p (z g t n) -> p z g t n", z=2, t=T, n=n)
+                nc.vector.tensor_copy(out=words[:, :, :, t0:t0 + 4],
+                                      in_=src[:].bitcast(I32).rearrange("p (f z g n) -> p z g f n", f=4, z=2, n=n))
+
         def code_moves(z, q, f0=0, nf=4):
             words = hb_codes[(q // 2) % 2][:, cols(8 * z, 8)].bitcast(I32)
             src = ha_codes[q % HA][:].bitcast(I32).rearrange("p (f z a g c) -> p z g a f c", f=4, z=2, a=4, g=8)[:, z]
@@ -176,15 +185,14 @@ def tile_higcin_volleyball_pa_t_kernel(tc, x, Wtheta, Wphi, out_0, out_1):
                 dst = words.rearrange("p (g t a c) -> p g a t c", g=8, t=T, a=4)
             moves(src, dst, q, f0, nf)
 
-        def scale_moves(q, f0=0, nf=4):
-            for z in range(2):
-                words = hb_scales[(q // 2) % 2][:, cols(8 * z, 8)].bitcast(I32)
-                src = ha_scales[q % HA][:].bitcast(I32).rearrange("p (f z a g) -> p z g a f", f=4, z=2, a=4)[:, z]
-                if z == 0:
-                    dst = words.rearrange("p (g a t) -> p g a t", g=8, t=T)
-                else:
-                    dst = words.rearrange("p (g t a) -> p g a t", g=8, t=T)
-                moves(src, dst, q, f0, nf)
+        def scale_moves(z, q, f0=0, nf=4):
+            words = hb_scales[(q // 2) % 2][:, cols(8 * z, 8)].bitcast(I32)
+            src = ha_scales[q % HA][:].bitcast(I32).rearrange("p (f z a g) -> p z g a f", f=4, z=2, a=4)[:, z]
+            if z == 0:
+                dst = words.rearrange("p (g a t) -> p g a t", g=8, t=T)
+            else:
+                dst = words.rearrange("p (g t a) -> p g a t", g=8, t=T)
+            moves(src, dst, q, f0, nf)
 
         def sw_pass(f, bank):
             s, fi = (f // 4) % HA, f % 4
@@ -198,9 +206,21 @@ def tile_higcin_volleyball_pa_t_kernel(tc, x, Wtheta, Wphi, out_0, out_1):
                 stop=True,
             )
 
-        def sw_out(q, bank, g0, n):
-            nc.scalar.mul(out=sw_sb[q % 4][:, g0:g0 + n].rearrange("p f (c m) -> p f c m", c=4),
-                          in_=bank[:, g0:g0 + n].rearrange("p f (m c) -> p f c m", c=4), mul=1.0 / N)
+        def sw_out(q, bank, g0, n, on_vector=False):
+            last = 4 * q // T == B - 1
+            dst = sw_sb[q % 4][:, g0:g0 + n]
+            src = bank[:, g0:g0 + n]
+            if last:
+                dst = dst.rearrange("p f (c m) -> p f c m", c=4)
+                src = src.rearrange("p f (m c) -> p f c m", c=4)
+            if on_vector:
+                nc.vector.tensor_scalar_mul(out=dst, in0=src, scalar1=1.0 / N)
+            else:
+                nc.scalar.mul(out=dst, in_=src, mul=1.0 / N)
+            if not last:
+                t0 = (4 * q + g0) % T
+                nc.sync.dma_start(out=out_0[4 * q // T, t0:t0 + n].rearrange("f j k -> j f k"), in_=sw_sb[q % 4][:, g0:g0 + n])
+                return
             for f in range(4 * q + g0, 4 * q + g0 + n):
                 nc.sync.dma_start(out=out_0[f // T, f % T].rearrange("(c m) k -> m c k", c=4), in_=sw_sb[q % 4][:, f % 4, :])
 
@@ -223,10 +243,9 @@ def tile_higcin_volleyball_pa_t_kernel(tc, x, Wtheta, Wphi, out_0, out_1):
                           in_=bank[:].rearrange("p g (s n) -> p n g s", n=16), mul=1.0 / T)
 
         def tw_store(b):
-            rows = out_1[b].rearrange("t (c a g) s -> a c t (g s)", c=4, a=4)
-            for a in range(4):
-                for c in range(4):
-                    nc.sync.dma_start(out=rows[a, c], in_=tw_sb[b % 2][32 * a + c:32 * a + 32:4, 4 * a + c].rearrange("p g s -> p (g s)"))
+            rows = out_1[b].rearrange("t (g n) s -> n t g s", n=16)
+            for n in range(16):
+                nc.sync.dma_start(out=rows[n], in_=tw_sb[b % 2][n:P:16, n])
 
         def tw_evac_last(half, bank, on_vector):
             for a in range(4):
@@ -243,12 +262,13 @@ def tile_higcin_volleyball_pa_t_kernel(tc, x, Wtheta, Wphi, out_0, out_1):
             for c in range(4):
                 nc.sync.dma_start(out=rows[c], in_=tw_last[c:P:4, c].rearrange("p g s -> p (g s)"))
 
-        w_transposes(0, (0, 1, 2, 3))
+        for u in range(4):
+            w_transposes(0, u, banks[u])
         evac_words(False, w_grp[0], 0, banks[0])
         evac_words(True, w_grp[0], 1, banks[1])
         evac_words(False, w_grp[0], 2, banks[2])
         quantise(w_codes[0], w_scales[0], w_grp[0], 0, 4)
-        evac_words(True, w_grp[0], 3, banks[3])
+        evac_words(False, w_grp[0], 3, banks[3])
         for f in range(4):
             x_transposes(f, banks[4 + f])
         evac_words(False, x_grp[0], 0, banks[4])
@@ -256,7 +276,7 @@ def tile_higcin_volleyball_pa_t_kernel(tc, x, Wtheta, Wphi, out_0, out_1):
         quantise(x_codes[0], x_scales[0], x_grp[0], 0, 2)
         evac_words(False, x_grp[0], 1, banks[5])
         evac_words(False, x_grp[0], 2, banks[6])
-        w_permute(0, False)
+        w_permute(0, True)
         quantise(x_codes[0], x_scales[0], x_grp[0], 2, 2)
         evac_words(True, x_grp[0], 3, banks[7])
         w_permute(1, False)
@@ -267,19 +287,20 @@ def tile_higcin_volleyball_pa_t_kernel(tc, x, Wtheta, Wphi, out_0, out_1):
         permute_frame(5, True)
         stage1(0, 0, banks[0], False)
         stage1(1, 0, banks[1], False)
-        w_transposes(1, (4, 5, 6, 7))
+        for u in range(4):
+            w_transposes(1, u, banks[4 + u])
         evac_words(True, w_grp[1], 0, banks[4])
         evac_words(False, w_grp[1], 1, banks[5])
         evac_words(True, w_grp[1], 2, banks[6])
         evac_words(False, w_grp[1], 3, banks[7])
         quantise(w_codes[1], w_scales[1], w_grp[1], 0, 4)
+        permute_frame(6, True)
+        permute_frame(7, True)
         stage1(2, 0, banks[2], False)
         stage1(3, 0, banks[3], False)
         quantise(w_codes[1], w_scales[1], w_grp[1], 4, 4)
-        for f in range(4, 6):
+        for f in range(4, 8):
             x_transposes_permuted(f, banks[f - 4])
-        for f in range(6, 8):
-            x_transposes(f, banks[f - 4])
         evac_words(True, x_grp[1], 0, banks[0])
         evac_words(False, x_grp[1], 1, banks[1])
         evac_words(True, x_grp[1], 2, banks[2])
@@ -300,15 +321,13 @@ def tile_higcin_volleyball_pa_t_kernel(tc, x, Wtheta, Wphi, out_0, out_1):
             evac_words(True, x_grp[s], 0, banks[0])
             h_quantise(2 * J - 1)
             evac_words(True, x_grp[s], 1, banks[1])
-            code_moves(0, J - 1)
             for k in range(2):
                 stage1(4 * J + k // 2, k % 2, banks[4 + k], False)
             for i in range(2, 4):
                 x_transposes_permuted(4 * nxt + i, banks[i])
             evac_words(False, x_grp[s], 2, banks[2])
-            evac_words(J % 2 == 0, x_grp[s], 3, banks[3])
-            code_moves(1, J - 1)
-            scale_moves(J - 1)
+            evac_words(True, x_grp[s], 3, banks[3])
+            quad_moves(J - 1)
             if J + 2 < QUADS:
                 permute_quad(J + 2)
             quantise(x_codes[s], x_scales[s], x_grp[s], 0, 4)
@@ -319,9 +338,10 @@ def tile_higcin_volleyball_pa_t_kernel(tc, x, Wtheta, Wphi, out_0, out_1):
                 for f in range(4 * J - 4, 4 * J):
                     sw_pass(f, banks[0])
                 sw_out(J - 1, banks[0], 0, 4)
-            helps = J == LASTQ - 1
+            helps_b = J == LASTQ - 1
+            helps_a = helps_b or J % 2 == 0
             for k in range(2):
-                stage1(4 * J + 2, k, banks[4 + k], helps and k == 1)
+                stage1(4 * J + 2, k, banks[4 + k], helps_a and k == 1)
             if (J - 1) % 2 == 1:
                 b = (J - 1) // 2
                 for half in range(2):
@@ -330,7 +350,7 @@ def tile_higcin_volleyball_pa_t_kernel(tc, x, Wtheta, Wphi, out_0, out_1):
                 tw_store(b)
             h_quantise(2 * J)
             for k in range(2):
-                stage1(4 * J + 3, k, banks[6 + k], helps and k == 1)
+                stage1(4 * J + 3, k, banks[6 + k], helps_b and k == 1)
 
         f0 = FRAMES - 4
         stage1(f0, 0, banks[4], False)
@@ -338,37 +358,36 @@ def tile_higcin_volleyball_pa_t_kernel(tc, x, Wtheta, Wphi, out_0, out_1):
         stage1(f0 + 1, 0, banks[6], False)
         h_quantise(2 * LASTQ - 1)
         code_moves(0, LASTQ - 1)
-        stage1(f0 + 1, 1, banks[7], True)
+        stage1(f0 + 1, 1, banks[7], False)
         code_moves(1, LASTQ - 1)
+        scale_moves(0, LASTQ - 1)
+        scale_moves(1, LASTQ - 1)
         stage1(f0 + 2, 0, banks[0], False)
         stage1(f0 + 2, 1, banks[1], False)
         h_quantise(2 * LASTQ)
         stage1(f0 + 3, 0, banks[2], False)
-        scale_moves(LASTQ - 1)
+        stage1(f0 + 3, 1, banks[3], False)
         code_moves(0, LASTQ, 0, 2)
-        code_moves(1, LASTQ, 0, 2)
-        scale_moves(LASTQ, 0, 2)
         h_quantise(2 * LASTQ + 1, 0, 2)
-        stage1(f0 + 3, 1, banks[3], True)
-        code_moves(0, LASTQ, 2, 1)
-        code_moves(1, LASTQ, 2, 1)
-        scale_moves(LASTQ, 2, 1)
-        h_quantise(2 * LASTQ + 1, 2, 2)
-        code_moves(0, LASTQ, 3, 1)
-        code_moves(1, LASTQ, 3, 1)
-        scale_moves(LASTQ, 3, 1)
-        for q in range(QUADS - 1 - LATE, LASTQ):
-            k = q - (QUADS - 1 - LATE)
+        code_moves(1, LASTQ, 0, 2)
+        h_quantise(2 * LASTQ + 1, 2, 1)
+        scale_moves(0, LASTQ, 0, 2)
+        scale_moves(1, LASTQ, 0, 2)
+        code_moves(0, LASTQ, 2, 2)
+        h_quantise(2 * LASTQ + 1, 3, 1)
+        scale_moves(0, LASTQ, 2, 2)
+        code_moves(1, LASTQ, 2, 2)
+        scale_moves(1, LASTQ, 2, 2)
+        for q in range(LASTQ - 1, QUADS - 2 - LATE, -1):
+            k = LASTQ - 1 - q
             for f in range(4 * q, 4 * q + 4):
                 sw_pass(f, banks[4 + k])
             sw_out(q, banks[4 + k], 0, 4)
-        for f in range(f0, f0 + 3):
-            sw_pass(f, banks[7])
-        for f in range(f0 + 3, FRAMES):
+        for f in range(f0, FRAMES):
             sw_pass(f, banks[7])
         for half in range(2):
             tw_passes(B - 1, half, banks[half])
-        sw_out(LASTQ, banks[7], 0, 4)
+        sw_out(LASTQ, banks[7], 0, 4, True)
         for half in range(2):
-            tw_evac_last(half, banks[half], half == 0)
+            tw_evac_last(half, banks[half], half == 1)
         tw_store_last(B - 1)

from contextlib import ExitStack

import concourse.masks as masks
import concourse.mybir as mybir

F32 = mybir.dt.float32
BF16 = mybir.dt.bfloat16
U32 = mybir.dt.uint32
I32 = mybir.dt.int32
U8 = mybir.dt.uint8
FP8X4 = mybir.dt.float8_e4m3fn_x4

P = 128
B, T, N, D, L = 4, 8, 128, 1024, 512
FRAMES = B * T
QUADS = FRAMES // 4
HA = 4
LATE = 2
FLOPS = 2 * 2 * FRAMES * N * D * L + 2 * FRAMES * N * N * L + 2 * B * N * T * T * L


def tile_higcin_volleyball_pa_t_kernel(tc, x, Wtheta, Wphi, out_0, out_1):
    nc = tc.nc
    with ExitStack() as ctx:
        keep = ctx.enter_context(tc.tile_pool(name="keep", bufs=1))
        psum = ctx.enter_context(tc.psum_pool(name="psum", bufs=1))
        ctx.enter_context(tc.manual_schedule())

        banks = [psum.tile([P, 4, P], F32, name="bank%d" % k) for k in range(8)]

        w_raw = [[keep.tile([P, D], BF16, name="w_raw%d%d" % (z, u)) for u in range(4)] for z in range(2)]
        w_perm = keep.tile([P, 4, D], BF16, name="w_perm")
        chunks = [(0, 1), (1, 1), (2, 1), (3, 1), (4, 2), (6, 2)] + [(f, 4) for f in range(8, FRAMES, 4)]
        x_raw = [keep.tile([P, n, D], BF16, name="x_raw%d" % f0) for (f0, n) in chunks]
        frame_src = {}
        for k, (f0, n) in enumerate(chunks):
            for i in range(n):
                frame_src[f0 + i] = (k, i)

        ident = keep.tile([P, P], F32, name="ident")

        w_grp = [keep.tile([P, 4, 2, P, 4], BF16, name="w_grp%d" % z, align_bytes=64) for z in range(2)]
        w_codes = [keep.tile([P, 8 * P], U32, name="w_codes%d" % z, align_bytes=64) for z in range(2)]
        w_scales = [keep.tile([P, 8 * P], U8, name="w_scales%d" % z, align_bytes=64) for z in range(2)]

        x_grp = [keep.tile([P, 4, 2, P, 4], BF16, name="x_grp%d" % k, align_bytes=64) for k in range(2)]
        x_codes = [keep.tile([P, 8 * P], U32, name="x_codes%d" % k, align_bytes=64) for k in range(2)]
        x_scales = [keep.tile([P, 8 * P], U8, name="x_scales%d" % k, align_bytes=64) for k in range(2)]

        h_grp = [keep.tile([P, 2, 2, P, 4], BF16, name="h_grp%d" % k, align_bytes=64) for k in range(3)]
        ha_codes = [keep.tile([P, 8 * P], U32, name="ha_codes%d" % k, align_bytes=64) for k in range(HA)]
        ha_scales = [keep.tile([P, 8 * P], U8, name="ha_scales%d" % k, align_bytes=64) for k in range(HA)]
        hb_codes = [keep.tile([P, 16 * P], U32, name="hb_codes%d" % k, align_bytes=64) for k in range(2)]
        hb_scales = [keep.tile([P, 16 * P], U8, name="hb_scales%d" % k, align_bytes=64) for k in range(2)]

        x_perm = [keep.tile([P, 4, D], BF16, name="x_perm%d" % k) for k in range(2)]

        sw_sb = [keep.tile([P, 4, P], F32, name="sw_sb%d" % k) for k in range(4)]
        tw_sb = [keep.tile([P, 16, 8, T], F32, name="tw_sb%d" % k) for k in range(2)]
        tw_last = keep.tile([P, 4, 8, T], F32, name="tw_last")

        xf = x.rearrange("b t j d -> j (b t) d")
        w_dram = [w.rearrange("(p u) d -> p u d", u=4) for w in (Wtheta, Wphi)]

        def load_w(z):
            for u in range(4):
                nc.sync.dma_start(out=w_raw[z][u][:], in_=w_dram[z][:, u, :])

        def load_x(k):
            f0, n = chunks[k]
            nc.sync.dma_start(out=x_raw[k][:], in_=xf[:, f0:f0 + n, :])

        load_w(0)
        for k in range(4):
            load_x(k)
        load_w(1)
        for k in range(4, len(chunks)):
            load_x(k)

        masks.make_identity(nc, ident[:])
        for k in range(HA):
            nc.vector.memset(ha_scales[k][:].bitcast(I32), 0)

        def cols(k, n=1):
            return slice(k * P, (k + n) * P)

        def transposes(bank, src):
            words = src.bitcast(F32)
            for c in range(2):
                for h in range(2):
                    nc.tensor.transpose(bank[:, 2 * c + h, :], words[:, 256 * c + h:256 * (c + 1):2], ident[:])

        def copy_out(on_vector, dst, src):
            if on_vector:
                nc.vector.tensor_copy(out=dst, in_=src)
            else:
                nc.scalar.copy(out=dst, in_=src)

        def evac_words(on_vector, grp, unit, bank):
            copy_out(on_vector, grp[:].bitcast(F32)[:, unit], bank[:].rearrange("p (c h) r -> p c r h", h=2))

        def quantise(codes, scales, grp, first, count):
            flat = grp[:].rearrange("p a b r t -> p (a b r t)")
            nc.vector.quantize_mx(out=codes[:, cols(first, count)].bitcast(FP8X4), scales=scales[:, cols(first, count)],
                                  in_=flat[:, 4 * P * first:4 * P * (first + count)])

        def permute_quad(q):
            k, i = frame_src[4 * q]
            for v in range(2):
                permute(True, x_perm[q % 2][:, 2 * v:2 * v + 2, :].rearrange("p f d -> p (f d)"),
                        x_raw[k][:, i + 2 * v:i + 2 * v + 2, :].rearrange("p f d -> p (f d)"))

        def x_transposes_permuted(f, bank):
            transposes_permuted(bank, x_perm[(f // 4) % 2][:, f % 4, :])

        def transposes_permuted(bank, src):
            words = src.bitcast(F32)
            for w in range(4):
                nc.tensor.transpose(bank[:, w, :], words[:, cols(w)], ident[:])

        def permute(on_vector, dst, src):
            copy_out(on_vector, dst.bitcast(F32).rearrange("p (c h w) -> p c h w", h=2, w=P),
                     src.bitcast(F32).rearrange("p (c w h) -> p c h w", h=2, w=P))

        def permute_frame(f, on_vector):
            k, i = frame_src[f]
            permute(on_vector, x_perm[(f // 4) % 2][:, f % 4, :], x_raw[k][:, i, :])

        def w_transposes(z, u, bank):
            if z == 0:
                transposes(bank, w_raw[0][u][:])
            else:
                transposes_permuted(bank, w_perm[:, u, :])

        def w_permute(u, on_vector):
            permute(on_vector, w_perm[:, u, :], w_raw[1][u][:])

        def x_transposes(f, bank):
            k, i = frame_src[f]
            transposes(bank, x_raw[k][:, i, :])

        def stage1(f, z, bank, on_vector):
            s = (f // 4) % 2
            for u in range(4):
                for c in range(2):
                    nc.tensor.matmul_mx(
                        out=bank[:, u, :],
                        lhsT=w_codes[z][:, cols(2 * u + c)].bitcast(FP8X4),
                        lhsT_scale=w_scales[z][:, cols(2 * u + c)],
                        rhs=x_codes[s][:, cols(2 * (f % 4) + c)].bitcast(FP8X4),
                        rhs_scale=x_scales[s][:, cols(2 * (f % 4) + c)],
                        start=(c == 0),
                        stop=(c == 1),
                    )
            dst = h_grp[(f // 2) % 3][:, f % 2, z]
            if f // T < B - 1:
                copy_out(on_vector, dst, bank[:].rearrange("p u n -> p n u"))
            else:
                copy_out(on_vector, dst.rearrange("p (m c) u -> p m c u", c=4), bank[:].rearrange("p u (c m) -> p m c u", c=4))

        def h_quantise(pair, first=0, count=4):
            q, at = pair // 2, 4 * (pair % 2)
            flat = h_grp[pair % 3][:].rearrange("p a b r t -> p (a b r t)")
            nc.vector.quantize_mx(out=ha_codes[q % HA][:, cols(at + first, count)].bitcast(FP8X4),
                                  scales=ha_scales[q % HA][:, cols(at + first, count)],
                                  in_=flat[:, 4 * P * first:4 * P * (first + count)])

        def moves(src, dst, q, f0, nf):
            t0 = 4 * (q % 2) + f0
            nc.vector.tensor_copy(out=dst[:, :, :, t0:t0 + nf], in_=src[:, :, :, f0:f0 + nf])

        def quad_moves(q):
            b, t0 = (q // 2) % 2, 4 * (q % 2)
            for (src, dst, n) in ((ha_codes[q % HA], hb_codes[b], 16), (ha_scales[q % HA], hb_scales[b], 4)):
                words = dst[:].bitcast(I32).rearrange("p (z g t n) -> p z g t n", z=2, t=T, n=n)
                nc.vector.tensor_copy(out=words[:, :, :, t0:t0 + 4],
                                      in_=src[:].bitcast(I32).rearrange("p (f z g n) -> p z g f n", f=4, z=2, n=n))

        def code_moves(z, q, f0=0, nf=4):
            words = hb_codes[(q // 2) % 2][:, cols(8 * z, 8)].bitcast(I32)
            src = ha_codes[q % HA][:].bitcast(I32).rearrange("p (f z a g c) -> p z g a f c", f=4, z=2, a=4, g=8)[:, z]
            if z == 0:
                dst = words.rearrange("p (g a t c) -> p g a t c", g=8, t=T, a=4)
            else:
                dst = words.rearrange("p (g t a c) -> p g a t c", g=8, t=T, a=4)
            moves(src, dst, q, f0, nf)

        def scale_moves(z, q, f0=0, nf=4):
            words = hb_scales[(q // 2) % 2][:, cols(8 * z, 8)].bitcast(I32)
            src = ha_scales[q % HA][:].bitcast(I32).rearrange("p (f z a g) -> p z g a f", f=4, z=2, a=4)[:, z]
            if z == 0:
                dst = words.rearrange("p (g a t) -> p g a t", g=8, t=T)
            else:
                dst = words.rearrange("p (g t a) -> p g a t", g=8, t=T)
            moves(src, dst, q, f0, nf)

        def sw_pass(f, bank):
            s, fi = (f // 4) % HA, f % 4
            nc.tensor.matmul_mx(
                out=bank[:, f % 4, :],
                lhsT=ha_codes[s][:, cols(2 * fi)].bitcast(FP8X4),
                lhsT_scale=ha_scales[s][:, cols(2 * fi)],
                rhs=ha_codes[s][:, cols(2 * fi + 1)].bitcast(FP8X4),
                rhs_scale=ha_scales[s][:, cols(2 * fi + 1)],
                start=True,
                stop=True,
            )

        def sw_out(q, bank, g0, n, on_vector=False):
            last = 4 * q // T == B - 1
            dst = sw_sb[q % 4][:, g0:g0 + n]
            src = bank[:, g0:g0 + n]
            if last:
                dst = dst.rearrange("p f (c m) -> p f c m", c=4)
                src = src.rearrange("p f (m c) -> p f c m", c=4)
            if on_vector:
                nc.vector.tensor_scalar_mul(out=dst, in0=src, scalar1=1.0 / N)
            else:
                nc.scalar.mul(out=dst, in_=src, mul=1.0 / N)
            if not last:
                t0 = (4 * q + g0) % T
                nc.sync.dma_start(out=out_0[4 * q // T, t0:t0 + n].rearrange("f j k -> j f k"), in_=sw_sb[q % 4][:, g0:g0 + n])
                return
            for f in range(4 * q + g0, 4 * q + g0 + n):
                nc.sync.dma_start(out=out_0[f // T, f % T].rearrange("(c m) k -> m c k", c=4), in_=sw_sb[q % 4][:, f % 4, :])

        def tw_passes(b, half, bank):
            s = b % 2
            for gg in range(4):
                g = 4 * half + gg
                nc.tensor.matmul_mx(
                    out=bank[:, gg, :],
                    lhsT=hb_codes[s][:, cols(g)].bitcast(FP8X4),
                    lhsT_scale=hb_scales[s][:, cols(g)],
                    rhs=hb_codes[s][:, cols(8 + g)].bitcast(FP8X4),
                    rhs_scale=hb_scales[s][:, cols(8 + g)],
                    start=True,
                    stop=True,
                )

        def tw_evac(b, half, bank):
            nc.scalar.mul(out=tw_sb[b % 2][:, :, 4 * half:4 * half + 4, :],
                          in_=bank[:].rearrange("p g (s n) -> p n g s", n=16), mul=1.0 / T)

        def tw_store(b):
            rows = out_1[b].rearrange("t (g n) s -> n t g s", n=16)
            for n in range(16):
                nc.sync.dma_start(out=rows[n], in_=tw_sb[b % 2][n:P:16, n])

        def tw_evac_last(half, bank, on_vector):
            for a in range(4):
                q = slice(32 * a, 32 * a + 32)
                dst = tw_last[q, :, 4 * half:4 * half + 4, :]
                src = bank[q].rearrange("p g (s a c) -> p a c g s", a=4, c=4)[:, a]
                if on_vector:
                    nc.vector.tensor_scalar_mul(out=dst, in0=src, scalar1=1.0 / T)
                else:
                    nc.scalar.mul(out=dst, in_=src, mul=1.0 / T)

        def tw_store_last(b):
            rows = out_1[b].rearrange("t (c a g) s -> c a t (g s)", c=4, a=4)
            for c in range(4):
                nc.sync.dma_start(out=rows[c], in_=tw_last[c:P:4, c].rearrange("p g s -> p (g s)"))

        for u in range(4):
            w_transposes(0, u, banks[u])
        evac_words(False, w_grp[0], 0, banks[0])
        evac_words(True, w_grp[0], 1, banks[1])
        evac_words(False, w_grp[0], 2, banks[2])
        quantise(w_codes[0], w_scales[0], w_grp[0], 0, 4)
        evac_words(False, w_grp[0], 3, banks[3])
        for f in range(4):
            x_transposes(f, banks[4 + f])
        evac_words(False, x_grp[0], 0, banks[4])
        quantise(w_codes[0], w_scales[0], w_grp[0], 4, 4)
        quantise(x_codes[0], x_scales[0], x_grp[0], 0, 2)
        evac_words(False, x_grp[0], 1, banks[5])
        evac_words(False, x_grp[0], 2, banks[6])
        w_permute(0, True)
        quantise(x_codes[0], x_scales[0], x_grp[0], 2, 2)
        evac_words(True, x_grp[0], 3, banks[7])
        w_permute(1, False)
        w_permute(2, True)
        w_permute(3, True)
        quantise(x_codes[0], x_scales[0], x_grp[0], 4, 4)
        permute_frame(4, True)
        permute_frame(5, True)
        stage1(0, 0, banks[0], False)
        stage1(1, 0, banks[1], False)
        for u in range(4):
            w_transposes(1, u, banks[4 + u])
        evac_words(True, w_grp[1], 0, banks[4])
        evac_words(False, w_grp[1], 1, banks[5])
        evac_words(True, w_grp[1], 2, banks[6])
        evac_words(False, w_grp[1], 3, banks[7])
        quantise(w_codes[1], w_scales[1], w_grp[1], 0, 4)
        permute_frame(6, True)
        permute_frame(7, True)
        stage1(2, 0, banks[2], False)
        stage1(3, 0, banks[3], False)
        quantise(w_codes[1], w_scales[1], w_grp[1], 4, 4)
        for f in range(4, 8):
            x_transposes_permuted(f, banks[f - 4])
        evac_words(True, x_grp[1], 0, banks[0])
        evac_words(False, x_grp[1], 1, banks[1])
        evac_words(True, x_grp[1], 2, banks[2])
        quantise(x_codes[1], x_scales[1], x_grp[1], 0, 4)
        evac_words(False, x_grp[1], 3, banks[3])
        for f in range(4):
            stage1(f, 1, banks[4 + f], False)
        permute_quad(2)
        quantise(x_codes[1], x_scales[1], x_grp[1], 4, 4)
        h_quantise(0)

        LASTQ = QUADS - 1
        for J in range(1, LASTQ):
            nxt = J + 1
            s = nxt % 2
            for i in range(2):
                x_transposes_permuted(4 * nxt + i, banks[i])
            evac_words(True, x_grp[s], 0, banks[0])
            h_quantise(2 * J - 1)
            evac_words(True, x_grp[s], 1, banks[1])
            for k in range(2):
                stage1(4 * J + k // 2, k % 2, banks[4 + k], False)
            for i in range(2, 4):
                x_transposes_permuted(4 * nxt + i, banks[i])
            evac_words(False, x_grp[s], 2, banks[2])
            evac_words(True, x_grp[s], 3, banks[3])
            quad_moves(J - 1)
            if J + 2 < QUADS:
                permute_quad(J + 2)
            quantise(x_codes[s], x_scales[s], x_grp[s], 0, 4)
            quantise(x_codes[s], x_scales[s], x_grp[s], 4, 4)
            for k in range(2, 4):
                stage1(4 * J + k // 2, k % 2, banks[4 + k], False)
            if J - 1 < QUADS - 1 - LATE:
                for f in range(4 * J - 4, 4 * J):
                    sw_pass(f, banks[0])
                sw_out(J - 1, banks[0], 0, 4)
            helps_b = J == LASTQ - 1
            helps_a = helps_b or J % 2 == 0
            for k in range(2):
                stage1(4 * J + 2, k, banks[4 + k], helps_a and k == 1)
            if (J - 1) % 2 == 1:
                b = (J - 1) // 2
                for half in range(2):
                    tw_passes(b, half, banks[1 + half])
                    tw_evac(b, half, banks[1 + half])
                tw_store(b)
            h_quantise(2 * J)
            for k in range(2):
                stage1(4 * J + 3, k, banks[6 + k], helps_b and k == 1)

        f0 = FRAMES - 4
        stage1(f0, 0, banks[4], False)
        stage1(f0, 1, banks[5], False)
        stage1(f0 + 1, 0, banks[6], False)
        h_quantise(2 * LASTQ - 1)
        code_moves(0, LASTQ - 1)
        stage1(f0 + 1, 1, banks[7], False)
        code_moves(1, LASTQ - 1)
        scale_moves(0, LASTQ - 1)
        scale_moves(1, LASTQ - 1)
        stage1(f0 + 2, 0, banks[0], False)
        stage1(f0 + 2, 1, banks[1], False)
        h_quantise(2 * LASTQ)
        stage1(f0 + 3, 0, banks[2], False)
        stage1(f0 + 3, 1, banks[3], False)
        code_moves(0, LASTQ, 0, 2)
        h_quantise(2 * LASTQ + 1, 0, 2)
        code_moves(1, LASTQ, 0, 2)
        h_quantise(2 * LASTQ + 1, 2, 1)
        scale_moves(0, LASTQ, 0, 2)
        scale_moves(1, LASTQ, 0, 2)
        code_moves(0, LASTQ, 2, 2)
        h_quantise(2 * LASTQ + 1, 3, 1)
        scale_moves(0, LASTQ, 2, 2)
        code_moves(1, LASTQ, 2, 2)
        scale_moves(1, LASTQ, 2, 2)
        for q in range(LASTQ - 1, QUADS - 2 - LATE, -1):
            k = LASTQ - 1 - q
            for f in range(4 * q, 4 * q + 4):
                sw_pass(f, banks[4 + k])
            sw_out(q, banks[4 + k], 0, 4)
        for f in range(f0, FRAMES):
            sw_pass(f, banks[7])
        for half in range(2):
            tw_passes(B - 1, half, banks[half])
        sw_out(LASTQ, banks[7], 0, 4, True)
        for half in range(2):
            tw_evac_last(half, banks[half], half == 1)
        tw_store_last(B - 1)
